import numpy as np
import ml_dtypes


def mxq(x, axis, fmt="e4m3"):
    dtype, down = {"e4m3": (ml_dtypes.float8_e4m3fn, 7), "e5m2": (ml_dtypes.float8_e5m2, 14)}[fmt]
    v = np.moveaxis(np.asarray(x, np.float32).astype(ml_dtypes.bfloat16).astype(np.float64), axis, -1)
    blocks = v.reshape(v.shape[:-1] + (-1, 32))
    amax = np.abs(blocks).max(-1, keepdims=True)
    byte = np.maximum(np.where(amax > 0, np.frexp(amax)[1] - 1 + 127, 0) - down, 1)
    scale = np.exp2(byte - 127.0)
    codes = (blocks / scale).astype(np.float32).astype(dtype).astype(np.float64)
    return np.moveaxis((codes * scale).reshape(v.shape), -1, axis)


WIDE = False


def mx_kscale(k):
    if not WIDE:
        return np.ones(k)
    levels = np.array([10, -10, 5, -5, 0])
    a = np.random.permutation(np.resize(levels, k // 512 * 4)).reshape(k // 512, 4)
    idx = np.arange(k)
    return np.exp2(a[idx // 512, idx % 128 // 32])


BF16 = ml_dtypes.bfloat16


def bf(x):
    return np.asarray(x, np.float32).astype(BF16)


def f64(x):
    return np.asarray(x).astype(np.float64)


E2M1 = np.array([0.0, 0.5, 1.0, 1.5, 2.0, 3.0, 4.0, 6.0, -0.0, -0.5, -1.0, -1.5, -2.0, -3.0, -4.0, -6.0])


def pack_weight(w, fmt):
    k, n = w.shape
    w = f64(bf(w)).reshape(k // 32, 32, n)
    amax = np.abs(w).max(1)
    if fmt == "e4m3":
        byte = np.frexp(amax)[1] - 1 + 127 - 7
    else:
        mant, ex = np.frexp(amax / 6.0)
        byte = np.where(mant > 0.5, ex, ex - 1) + 127
    byte = np.clip(np.where(amax > 0, byte, 1), 1, 254)
    scaled = (w * np.exp2(127.0 - byte)[:, None, :]).reshape(k, n).astype(np.float32)
    by_word = np.ascontiguousarray(scaled.reshape(k // 512, 128, 4, n).transpose(0, 1, 3, 2))
    if fmt == "e4m3":
        words = by_word.astype(ml_dtypes.float8_e4m3fn).view(np.uint8)
    else:
        c = by_word.astype(ml_dtypes.float4_e2m1fn).view(np.uint8) & 0xF
        words = c[..., 0::2] | (c[..., 1::2] << 4)
    return np.ascontiguousarray(words), np.ascontiguousarray(byte.astype(np.uint8).reshape(k // 512, 16, n))


def unpack_weight(words, scales, fmt):
    g, p, n, _ = words.shape
    if fmt == "e4m3":
        vals = np.ascontiguousarray(words).view(ml_dtypes.float8_e4m3fn).astype(np.float64)
    else:
        nib = np.empty((g, p, n, 4), np.uint8)
        nib[..., 0::2] = words & 0xF
        nib[..., 1::2] = words >> 4
        vals = E2M1[nib]
    vals = vals * np.repeat(np.exp2(scales.astype(np.float64) - 127.0), 8, axis=1)[..., None]
    return vals.transpose(0, 1, 3, 2).reshape(g * 512, n)

def pack4(w):
    words, scales = pack_weight(w, "e2m1")
    return words.reshape(words.shape[0], 128, -1), scales


def unpack4(words, scales):
    return unpack_weight(words.reshape(words.shape[0], 128, -1, 2), scales, "e2m1")


B, S, HID, H, HKV, DH = 4, 2048, 512, 2, 1, 64
NH = H + 2 * HKV


def rotate_half(x):
    x1 = x[..., ::2]
    x2 = x[..., 1::2]
    return np.stack((-x2, x1), axis=-1).reshape(x.shape)


def setup_inputs():
    s = mx_kscale(HID)
    inv_freq = 1.0 / (10000.0 ** (np.arange(0, DH, 2) / DH))
    emb = np.repeat(np.outer(np.arange(S), inv_freq), 2, axis=-1)
    hidden_states = bf(np.random.standard_normal((B, S, HID)) * s)
    cos = bf(np.cos(emb))
    sin = bf(np.sin(emb))
    w = np.random.standard_normal((NH * DH, HID)) / np.sqrt(HID) / s[None, :]
    words, scales = pack4(np.ascontiguousarray(w.T))
    return {"hidden_states": hidden_states,
            "cos": cos,
            "sin": sin,
            "w_qkv_words": words,
            "w_qkv_scales": scales}


def reference(hidden_states, cos, sin, w_qkv_words, w_qkv_scales):
    qkv = mxq(f64(hidden_states), 2, "e4m3") @ unpack4(w_qkv_words, w_qkv_scales)
    qkv = qkv.reshape(B, S, NH, DH)
    q = qkv[:, :, :H]
    k = qkv[:, :, H:H + HKV]
    v = qkv[:, :, H + HKV:]
    cos_s = f64(cos)[:S][None, :, None, :]
    sin_s = f64(sin)[:S][None, :, None, :]
    q = q * cos_s + rotate_half(q) * sin_s
    k = k * cos_s + rotate_half(k) * sin_s
    return q, k, v

@@ -1,0 +1,207 @@
+from contextlib import ExitStack
+
+import concourse.mybir as mybir
+from concourse.masks import make_identity
+
+BF16 = mybir.dt.bfloat16
+F32 = mybir.dt.float32
+I32 = mybir.dt.int32
+U8 = mybir.dt.uint8
+U32 = mybir.dt.uint32
+FP8X4 = mybir.dt.float8_e4m3fn_x4
+FP4X4 = mybir.dt.float4_e2m1fn_x4
+MULT = mybir.AluOpType.mult
+ADD = mybir.AluOpType.add
+
+P = 128
+BATCH = 4
+SEQ = 2048
+HIDDEN = 512
+LANES = 64
+ROPE_HEADS = 3
+Q_COLS = 2 * LANES
+ROPE_COLS = ROPE_HEADS * LANES
+OUT_COLS = 4 * LANES
+PAIRS = LANES // 2
+
+SLOTS = SEQ // P
+ROUND_TILES = 4
+BANK_TILES = 2
+ROUND_BANKS = ROUND_TILES // BANK_TILES
+ROUNDS_PER_BATCH = SLOTS // ROUND_TILES
+ROUNDS = BATCH * ROUNDS_PER_BATCH
+
+FLOPS = 2 * BATCH * SEQ * HIDDEN * OUT_COLS
+
+
+def tile_attention_pa_t_kernel(
+    tc, hidden_states, cos, sin, w_qkv_words, w_qkv_scales, out_0, out_1, out_2
+):
+    nc = tc.nc
+
+    x_view = hidden_states.rearrange("b (p t) k -> b p t k", t=SLOTS)
+    q_view = out_0.rearrange("b (p t) h d -> b p t (h d)", t=SLOTS)
+    k_view = out_1.rearrange("b (p t) h d -> b p t (h d)", t=SLOTS)
+    v_view = out_2.rearrange("b (p t) h d -> b p t (h d)", t=SLOTS)
+    cos_view = cos.rearrange("(p t) d -> p t d", t=SLOTS)
+    sin_view = sin.rearrange("(p t) d -> p t d", t=SLOTS)
+
+    with ExitStack() as ctx:
+        const = ctx.enter_context(tc.tile_pool(name="const", bufs=1))
+        x_pool = ctx.enter_context(tc.tile_pool(name="x", bufs=ROUNDS))
+        out_pool = ctx.enter_context(tc.tile_pool(name="out", bufs=ROUNDS))
+        work = ctx.enter_context(tc.tile_pool(name="work", bufs=3))
+        xt_pool = ctx.enter_context(tc.psum_pool(name="xt", bufs=2 * ROUND_BANKS))
+        acc_pool = ctx.enter_context(tc.psum_pool(name="acc", bufs=2 * ROUND_BANKS))
+
+        def batch_and_first_slot(r):
+            return r // ROUNDS_PER_BATCH, (r % ROUNDS_PER_BATCH) * ROUND_TILES
+
+        x_tiles = []
+
+        def load_x(r):
+            b, first = batch_and_first_slot(r)
+            x_sb = x_pool.tile([P, ROUND_TILES, HIDDEN], BF16, name="x_sb")
+            nc.sync.dma_start(out=x_sb[:], in_=x_view[b, :, first : first + ROUND_TILES, :])
+            x_tiles.append(x_sb)
+
+        w_plane = const.tile([P, OUT_COLS], U8, align_bytes=64)
+        nc.vector.memset(w_plane[:].bitcast(I32), 0)
+        ident = const.tile([P, P], F32)
+        make_identity(nc, ident[:])
+
+        load_x(0)
+        w_words = const.tile([P, 2 * OUT_COLS], U8, align_bytes=64)
+        nc.sync.dma_start(out=w_words[:].bitcast(I32), in_=w_qkv_words[0].bitcast(I32))
+        for quadrant in range(4):
+            nc.sync.dma_start(
+                out=w_plane[32 * quadrant : 32 * quadrant + 4, :].bitcast(I32),
+                in_=w_qkv_scales[0, 4 * quadrant : 4 * quadrant + 4, :].bitcast(I32),
+            )
+        load_x(1)
+
+        by_even = const.tile([P, SLOTS, LANES], BF16)
+        by_odd = const.tile([P, SLOTS, LANES], BF16)
+        sin_sb = const.tile([P, SLOTS, LANES], BF16)
+        nc.sync.dma_start(out=by_even[:], in_=cos_view)
+        nc.sync.dma_start(out=by_odd[:], in_=cos_view)
+        nc.sync.dma_start(out=sin_sb[:], in_=sin_view)
+        sin_pairs = sin_sb[:].rearrange("p t (i two) -> p t i two", two=2)
+        nc.vector.tensor_copy(
+            out=by_even[:].rearrange("p t (i two) -> p t i two", two=2)[:, :, :, 1],
+            in_=sin_pairs[:, :, :, 1],
+        )
+        nc.vector.tensor_scalar_mul(
+            out=by_odd[:].rearrange("p t (i two) -> p t i two", two=2)[:, :, :, 0],
+            in0=sin_pairs[:, :, :, 0],
+            scalar1=-1.0,
+        )
+        for r in range(2, ROUNDS):
+            load_x(r)
+
+        grouped_tiles = {}
+        code_tiles = {}
+        acc_tiles = {}
+
+        def transpose_and_regroup(r):
+            x_words = x_tiles[r][:].bitcast(F32)
+            grouped = work.tile([P, ROUND_TILES, P, 4], BF16, name="grouped", align_bytes=64)
+            grouped_words = (
+                grouped[:]
+                .rearrange("p a r j -> p a (r j)")
+                .bitcast(F32)
+                .rearrange("p a (r u) -> p a r u", u=2)
+            )
+            for bank in range(ROUND_BANKS):
+                xt = xt_pool.tile([P, BANK_TILES, 2, P], F32, name="xt")
+                for a in range(BANK_TILES):
+                    for u in range(2):
+                        nc.tensor.transpose(
+                            xt[:, a, u, :],
+                            x_words[:, bank * BANK_TILES + a, u : HIDDEN // 2 : 2],
+                            ident[:],
+                        )
+                nc.scalar.copy(
+                    out=grouped_words[:, bank * BANK_TILES : (bank + 1) * BANK_TILES, :, :],
+                    in_=xt[:].rearrange("p a u r -> p a r u"),
+                )
+            grouped_tiles[r] = grouped
+
+        def quantise(r):
+            codes = work.tile([P, ROUND_TILES * P], U32, name="codes", align_bytes=64)
+            x_plane = work.tile([P, ROUND_TILES * P], U8, name="x_plane", align_bytes=64)
+            nc.vector.quantize_mx(
+                out=codes[:].bitcast(FP8X4),
+                scales=x_plane[:],
+                in_=grouped_tiles.pop(r)[:].rearrange("p a r j -> p (a r j)"),
+            )
+            code_tiles[r] = (codes, x_plane)
+
+        def multiply(r):
+            codes, x_plane = code_tiles.pop(r)
+            banks = []
+            for bank in range(ROUND_BANKS):
+                acc = acc_pool.tile([P, BANK_TILES, OUT_COLS], F32, name="acc")
+                for a in range(BANK_TILES):
+                    tokens = slice((bank * BANK_TILES + a) * P, (bank * BANK_TILES + a + 1) * P)
+                    nc.tensor.matmul_mx(
+                        out=acc[:, a, :],
+                        lhsT=codes[:, tokens].bitcast(FP8X4),
+                        lhsT_scale=x_plane[:, tokens],
+                        rhs=w_words[:].bitcast(FP4X4),
+                        rhs_scale=w_plane[:],
+                        start=True,
+                        stop=True,
+                    )
+                banks.append(acc)
+            acc_tiles[r] = banks
+
+        def rotate_and_store(r):
+            b, first = batch_and_first_slot(r)
+            slots = slice(first, first + ROUND_TILES)
+            shape = [P, BANK_TILES, ROPE_HEADS, PAIRS, 2]
+            from_even = work.tile([P, ROUND_TILES, ROPE_COLS], F32, name="from_even")
+            from_odd = work.tile([P, ROUND_TILES, ROPE_COLS], F32, name="from_odd")
+            q_sb = out_pool.tile([P, ROUND_TILES, Q_COLS], F32, name="q_sb")
+            k_sb = out_pool.tile([P, ROUND_TILES, LANES], F32, name="k_sb")
+            v_sb = out_pool.tile([P, ROUND_TILES, LANES], F32, name="v_sb")
+            for bank, acc in enumerate(acc_tiles.pop(r)):
+                tiles = slice(bank * BANK_TILES, (bank + 1) * BANK_TILES)
+                table_slots = slice(first + bank * BANK_TILES, first + (bank + 1) * BANK_TILES)
+                pairs = acc[:, :, 0:ROPE_COLS].rearrange(
+                    "p a (h i two) -> p a h i two", h=ROPE_HEADS, two=2
+                )
+                for lane, table, product in ((0, by_even, from_even), (1, by_odd, from_odd)):
+                    nc.vector.tensor_tensor(
+                        out=product[:, tiles, :].rearrange(
+                            "p a (h i two) -> p a h i two", h=ROPE_HEADS, two=2
+                        ),
+                        in0=pairs[:, :, :, :, lane : lane + 1].broadcast_to(shape),
+                        in1=table[:, table_slots, :]
+                        .rearrange("p a (i two) -> p a i two", two=2)
+                        .unsqueeze(2)
+                        .broadcast_to(shape),
+                        op=MULT,
+                    )
+                nc.vector.tensor_copy(out=v_sb[:, tiles, :], in_=acc[:, :, ROPE_COLS:OUT_COLS])
+            nc.gpsimd.tensor_tensor(
+                out=q_sb[:], in0=from_even[:, :, 0:Q_COLS], in1=from_odd[:, :, 0:Q_COLS], op=ADD
+            )
+            nc.gpsimd.tensor_tensor(
+                out=k_sb[:],
+                in0=from_even[:, :, Q_COLS:ROPE_COLS],
+                in1=from_odd[:, :, Q_COLS:ROPE_COLS],
+                op=ADD,
+            )
+            nc.sync.dma_start(out=v_view[b, :, slots, :], in_=v_sb[:])
+            nc.sync.dma_start(out=q_view[b, :, slots, :], in_=q_sb[:])
+            nc.sync.dma_start(out=k_view[b, :, slots, :], in_=k_sb[:])
+
+        for step in range(ROUNDS + 2):
+            if step < ROUNDS:
+                transpose_and_regroup(step)
+            if 1 <= step <= ROUNDS:
+                quantise(step - 1)
+                multiply(step - 1)
+            if step >= 2:
+                rotate_and_store(step - 2)

@@ -18,10 +18,11 @@ BATCH = 4
 SEQ = 2048
 HIDDEN = 512
 LANES = 64
-ROPE_HEADS = 3
-Q_COLS = 2 * LANES
-ROPE_COLS = ROPE_HEADS * LANES
-OUT_COLS = 4 * LANES
+Q_HEADS = 2
+Q_COLS = Q_HEADS * LANES
+K_START = Q_COLS
+V_START = Q_COLS + LANES
+OUT_COLS = Q_COLS + 2 * LANES
 PAIRS = LANES // 2
 
 SLOTS = SEQ // P
@@ -51,8 +52,8 @@ def tile_attention_pa_t_kernel(
         x_pool = ctx.enter_context(tc.tile_pool(name="x", bufs=ROUNDS))
         out_pool = ctx.enter_context(tc.tile_pool(name="out", bufs=ROUNDS))
         work = ctx.enter_context(tc.tile_pool(name="work", bufs=3))
-        xt_pool = ctx.enter_context(tc.psum_pool(name="xt", bufs=2 * ROUND_BANKS))
-        acc_pool = ctx.enter_context(tc.psum_pool(name="acc", bufs=2 * ROUND_BANKS))
+        xt_pool = ctx.enter_context(tc.psum_pool(name="xt", bufs=ROUND_BANKS))
+        acc_pool = ctx.enter_context(tc.psum_pool(name="acc", bufs=2))
 
         def batch_and_first_slot(r):
             return r // ROUNDS_PER_BATCH, (r % ROUNDS_PER_BATCH) * ROUND_TILES
@@ -139,63 +140,58 @@ def tile_attention_pa_t_kernel(
 
         def multiply(r):
             codes, x_plane = code_tiles.pop(r)
-            banks = []
-            for bank in range(ROUND_BANKS):
-                acc = acc_pool.tile([P, BANK_TILES, OUT_COLS], F32, name="acc")
-                for a in range(BANK_TILES):
-                    tokens = slice((bank * BANK_TILES + a) * P, (bank * BANK_TILES + a + 1) * P)
+            q_acc = acc_pool.tile([P, ROUND_TILES, Q_COLS], F32, name="q_acc")
+            k_acc = acc_pool.tile([P, ROUND_TILES, LANES], F32, name="k_acc")
+            v_acc = acc_pool.tile([P, ROUND_TILES, LANES], F32, name="v_acc")
+            for acc, first_col, cols in (
+                (q_acc, 0, Q_COLS),
+                (k_acc, K_START, LANES),
+                (v_acc, V_START, LANES),
+            ):
+                for a in range(ROUND_TILES):
                     nc.tensor.matmul_mx(
                         out=acc[:, a, :],
-                        lhsT=codes[:, tokens].bitcast(FP8X4),
-                        lhsT_scale=x_plane[:, tokens],
-                        rhs=w_words[:].bitcast(FP4X4),
-                        rhs_scale=w_plane[:],
+                        lhsT=codes[:, a * P : (a + 1) * P].bitcast(FP8X4),
+                        lhsT_scale=x_plane[:, a * P : (a + 1) * P],
+                        rhs=w_words[:, 2 * first_col : 2 * (first_col + cols)].bitcast(FP4X4),
+                        rhs_scale=w_plane[:, first_col : first_col + cols],
                         start=True,
                         stop=True,
                     )
-                banks.append(acc)
-            acc_tiles[r] = banks
+            acc_tiles[r] = (q_acc, k_acc, v_acc)
 
         def rotate_and_store(r):
             b, first = batch_and_first_slot(r)
             slots = slice(first, first + ROUND_TILES)
-            shape = [P, BANK_TILES, ROPE_HEADS, PAIRS, 2]
-            from_even = work.tile([P, ROUND_TILES, ROPE_COLS], F32, name="from_even")
-            from_odd = work.tile([P, ROUND_TILES, ROPE_COLS], F32, name="from_odd")
-            q_sb = out_pool.tile([P, ROUND_TILES, Q_COLS], F32, name="q_sb")
-            k_sb = out_pool.tile([P, ROUND_TILES, LANES], F32, name="k_sb")
+            q_acc, k_acc, v_acc = acc_tiles.pop(r)
+
             v_sb = out_pool.tile([P, ROUND_TILES, LANES], F32, name="v_sb")
-            for bank, acc in enumerate(acc_tiles.pop(r)):
-                tiles = slice(bank * BANK_TILES, (bank + 1) * BANK_TILES)
-                table_slots = slice(first + bank * BANK_TILES, first + (bank + 1) * BANK_TILES)
-                pairs = acc[:, :, 0:ROPE_COLS].rearrange(
-                    "p a (h i two) -> p a h i two", h=ROPE_HEADS, two=2
-                )
-                for lane, table, product in ((0, by_even, from_even), (1, by_odd, from_odd)):
+            nc.scalar.copy(out=v_sb[:], in_=v_acc[:])
+            nc.sync.dma_start(out=v_view[b, :, slots, :], in_=v_sb[:])
+
+            for acc, heads, view, label in ((q_acc, Q_HEADS, q_view, "q"), (k_acc, 1, k_view, "k")):
+                shape = [P, ROUND_TILES, heads, PAIRS, 2]
+                pairs = acc[:].rearrange("p a (h i two) -> p a h i two", h=heads, two=2)
+                products = []
+                for lane, table in ((0, by_even), (1, by_odd)):
+                    product = work.tile(
+                        [P, ROUND_TILES, heads * LANES], F32, name="%s_product_%d" % (label, lane)
+                    )
                     nc.vector.tensor_tensor(
-                        out=product[:, tiles, :].rearrange(
-                            "p a (h i two) -> p a h i two", h=ROPE_HEADS, two=2
-                        ),
+                        out=product[:].rearrange("p a (h i two) -> p a h i two", h=heads, two=2),
                         in0=pairs[:, :, :, :, lane : lane + 1].broadcast_to(shape),
-                        in1=table[:, table_slots, :]
+                        in1=table[:, slots, :]
                         .rearrange("p a (i two) -> p a i two", two=2)
                         .unsqueeze(2)
                         .broadcast_to(shape),
                         op=MULT,
                     )
-                nc.vector.tensor_copy(out=v_sb[:, tiles, :], in_=acc[:, :, ROPE_COLS:OUT_COLS])
-            nc.gpsimd.tensor_tensor(
-                out=q_sb[:], in0=from_even[:, :, 0:Q_COLS], in1=from_odd[:, :, 0:Q_COLS], op=ADD
-            )
-            nc.gpsimd.tensor_tensor(
-                out=k_sb[:],
-                in0=from_even[:, :, Q_COLS:ROPE_COLS],
-                in1=from_odd[:, :, Q_COLS:ROPE_COLS],
-                op=ADD,
-            )
-            nc.sync.dma_start(out=v_view[b, :, slots, :], in_=v_sb[:])
-            nc.sync.dma_start(out=q_view[b, :, slots, :], in_=q_sb[:])
-            nc.sync.dma_start(out=k_view[b, :, slots, :], in_=k_sb[:])
+                    products.append(product)
+                rotated = out_pool.tile([P, ROUND_TILES, heads * LANES], F32, name="%s_sb" % label)
+                nc.gpsimd.tensor_tensor(
+                    out=rotated[:], in0=products[0][:], in1=products[1][:], op=ADD
+                )
+                nc.sync.dma_start(out=view[b, :, slots, :], in_=rotated[:])
 
         for step in range(ROUNDS + 2):
             if step < ROUNDS:

@@ -21,7 +21,6 @@ LANES = 64
 Q_HEADS = 2
 Q_COLS = Q_HEADS * LANES
 K_START = Q_COLS
-V_START = Q_COLS + LANES
 OUT_COLS = Q_COLS + 2 * LANES
 PAIRS = LANES // 2
 
@@ -141,12 +140,12 @@ def tile_attention_pa_t_kernel(
         def multiply(r):
             codes, x_plane = code_tiles.pop(r)
             q_acc = acc_pool.tile([P, ROUND_TILES, Q_COLS], F32, name="q_acc")
-            k_acc = acc_pool.tile([P, ROUND_TILES, LANES], F32, name="k_acc")
-            v_acc = acc_pool.tile([P, ROUND_TILES, LANES], F32, name="v_acc")
+            k_acc = acc_pool.tile([P, ROUND_TILES, 2 * LANES], F32, name="k_acc")
+            v_acc = acc_pool.tile([P, ROUND_TILES, 2 * LANES], F32, name="v_acc")
             for acc, first_col, cols in (
                 (q_acc, 0, Q_COLS),
-                (k_acc, K_START, LANES),
-                (v_acc, V_START, LANES),
+                (k_acc, K_START, 2 * LANES),
+                (v_acc, K_START, 2 * LANES),
             ):
                 for a in range(ROUND_TILES):
                     nc.tensor.matmul_mx(
@@ -166,12 +165,14 @@ def tile_attention_pa_t_kernel(
             q_acc, k_acc, v_acc = acc_tiles.pop(r)
 
             v_sb = out_pool.tile([P, ROUND_TILES, LANES], F32, name="v_sb")
-            nc.scalar.copy(out=v_sb[:], in_=v_acc[:])
+            nc.scalar.copy(out=v_sb[:], in_=v_acc[:, :, LANES : 2 * LANES])
             nc.sync.dma_start(out=v_view[b, :, slots, :], in_=v_sb[:])
 
             for acc, heads, view, label in ((q_acc, Q_HEADS, q_view, "q"), (k_acc, 1, k_view, "k")):
                 shape = [P, ROUND_TILES, heads, PAIRS, 2]
-                pairs = acc[:].rearrange("p a (h i two) -> p a h i two", h=heads, two=2)
+                pairs = acc[:, :, 0 : heads * LANES].rearrange(
+                    "p a (h i two) -> p a h i two", h=heads, two=2
+                )
                 products = []
                 for lane, table in ((0, by_even), (1, by_odd)):
                     product = work.tile(

@@ -18,10 +18,10 @@ BATCH = 4
 SEQ = 2048
 HIDDEN = 512
 LANES = 64
-Q_HEADS = 2
-Q_COLS = Q_HEADS * LANES
-K_START = Q_COLS
-OUT_COLS = Q_COLS + 2 * LANES
+ROPE_HEADS = 3
+Q_COLS = 2 * LANES
+ROPE_COLS = ROPE_HEADS * LANES
+OUT_COLS = 4 * LANES
 PAIRS = LANES // 2
 
 SLOTS = SEQ // P
@@ -51,26 +51,31 @@ def tile_attention_pa_t_kernel(
         x_pool = ctx.enter_context(tc.tile_pool(name="x", bufs=ROUNDS))
         out_pool = ctx.enter_context(tc.tile_pool(name="out", bufs=ROUNDS))
         work = ctx.enter_context(tc.tile_pool(name="work", bufs=3))
-        xt_pool = ctx.enter_context(tc.psum_pool(name="xt", bufs=ROUND_BANKS))
-        acc_pool = ctx.enter_context(tc.psum_pool(name="acc", bufs=2))
+        xt_pool = ctx.enter_context(tc.psum_pool(name="xt", bufs=2 * ROUND_BANKS))
+        acc_pool = ctx.enter_context(tc.psum_pool(name="acc", bufs=2 * ROUND_BANKS))
 
         def batch_and_first_slot(r):
             return r // ROUNDS_PER_BATCH, (r % ROUNDS_PER_BATCH) * ROUND_TILES
 
         x_tiles = []
 
-        def load_x(r):
+        def load_x(r, bank):
             b, first = batch_and_first_slot(r)
-            x_sb = x_pool.tile([P, ROUND_TILES, HIDDEN], BF16, name="x_sb")
-            nc.sync.dma_start(out=x_sb[:], in_=x_view[b, :, first : first + ROUND_TILES, :])
-            x_tiles.append(x_sb)
+            if bank == 0:
+                x_sb = x_pool.tile([P, ROUND_TILES, HIDDEN], BF16, name="x_sb")
+                x_tiles.append(x_sb)
+            tiles = slice(bank * BANK_TILES, (bank + 1) * BANK_TILES)
+            slots = slice(first + bank * BANK_TILES, first + (bank + 1) * BANK_TILES)
+            nc.sync.dma_start(out=x_tiles[r][:, tiles, :], in_=x_view[b, :, slots, :])
 
         w_plane = const.tile([P, OUT_COLS], U8, align_bytes=64)
         nc.vector.memset(w_plane[:].bitcast(I32), 0)
         ident = const.tile([P, P], F32)
         make_identity(nc, ident[:])
 
-        load_x(0)
+        for r in range(2):
+            for bank in range(ROUND_BANKS):
+                load_x(r, bank)
         w_words = const.tile([P, 2 * OUT_COLS], U8, align_bytes=64)
         nc.sync.dma_start(out=w_words[:].bitcast(I32), in_=w_qkv_words[0].bitcast(I32))
         for quadrant in range(4):
@@ -78,26 +83,29 @@ def tile_attention_pa_t_kernel(
                 out=w_plane[32 * quadrant : 32 * quadrant + 4, :].bitcast(I32),
                 in_=w_qkv_scales[0, 4 * quadrant : 4 * quadrant + 4, :].bitcast(I32),
             )
-        load_x(1)
 
         by_even = const.tile([P, SLOTS, LANES], BF16)
         by_odd = const.tile([P, SLOTS, LANES], BF16)
+        cos_sb = const.tile([P, SLOTS, LANES], BF16)
         sin_sb = const.tile([P, SLOTS, LANES], BF16)
-        nc.sync.dma_start(out=by_even[:], in_=cos_view)
-        nc.sync.dma_start(out=by_odd[:], in_=cos_view)
         nc.sync.dma_start(out=sin_sb[:], in_=sin_view)
-        sin_pairs = sin_sb[:].rearrange("p t (i two) -> p t i two", two=2)
-        nc.vector.tensor_copy(
-            out=by_even[:].rearrange("p t (i two) -> p t i two", two=2)[:, :, :, 1],
-            in_=sin_pairs[:, :, :, 1],
-        )
-        nc.vector.tensor_scalar_mul(
-            out=by_odd[:].rearrange("p t (i two) -> p t i two", two=2)[:, :, :, 0],
-            in0=sin_pairs[:, :, :, 0],
-            scalar1=-1.0,
-        )
+        nc.sync.dma_start(out=cos_sb[:], in_=cos_view)
         for r in range(2, ROUNDS):
-            load_x(r)
+            for bank in range(ROUND_BANKS):
+                load_x(r, bank)
+
+        def lanes(table, lane):
+            return table[:].rearrange("p t (i two) -> p t i two", two=2)[:, :, :, lane]
+
+        def build_tables():
+            nc.vector.tensor_copy(out=lanes(by_even, 1), in_=lanes(sin_sb, 1))
+            nc.vector.tensor_copy(out=lanes(by_even, 0), in_=lanes(cos_sb, 0))
+            nc.gpsimd.tensor_scalar(
+                out=lanes(by_odd, 0), in0=lanes(sin_sb, 0), scalar1=-1.0, scalar2=0.0, op0=MULT, op1=ADD
+            )
+            nc.gpsimd.tensor_scalar(
+                out=lanes(by_odd, 1), in0=lanes(cos_sb, 1), scalar1=1.0, scalar2=0.0, op0=MULT, op1=ADD
+            )
 
         grouped_tiles = {}
         code_tiles = {}
@@ -130,75 +138,89 @@ def tile_attention_pa_t_kernel(
         def quantise(r):
             codes = work.tile([P, ROUND_TILES * P], U32, name="codes", align_bytes=64)
             x_plane = work.tile([P, ROUND_TILES * P], U8, name="x_plane", align_bytes=64)
-            nc.vector.quantize_mx(
-                out=codes[:].bitcast(FP8X4),
-                scales=x_plane[:],
-                in_=grouped_tiles.pop(r)[:].rearrange("p a r j -> p (a r j)"),
-            )
+            grouped = grouped_tiles.pop(r)
+            for bank in range(ROUND_BANKS):
+                tiles = slice(bank * BANK_TILES, (bank + 1) * BANK_TILES)
+                tokens = slice(bank * BANK_TILES * P, (bank + 1) * BANK_TILES * P)
+                nc.vector.quantize_mx(
+                    out=codes[:, tokens].bitcast(FP8X4),
+                    scales=x_plane[:, tokens],
+                    in_=grouped[:, tiles, :, :].rearrange("p a r j -> p (a r j)"),
+                )
             code_tiles[r] = (codes, x_plane)
 
         def multiply(r):
             codes, x_plane = code_tiles.pop(r)
-            q_acc = acc_pool.tile([P, ROUND_TILES, Q_COLS], F32, name="q_acc")
-            k_acc = acc_pool.tile([P, ROUND_TILES, 2 * LANES], F32, name="k_acc")
-            v_acc = acc_pool.tile([P, ROUND_TILES, 2 * LANES], F32, name="v_acc")
-            for acc, first_col, cols in (
-                (q_acc, 0, Q_COLS),
-                (k_acc, K_START, 2 * LANES),
-                (v_acc, K_START, 2 * LANES),
-            ):
-                for a in range(ROUND_TILES):
+            banks = []
+            for bank in range(ROUND_BANKS):
+                acc = acc_pool.tile([P, BANK_TILES, OUT_COLS], F32, name="acc")
+                for a in range(BANK_TILES):
+                    tokens = slice((bank * BANK_TILES + a) * P, (bank * BANK_TILES + a + 1) * P)
                     nc.tensor.matmul_mx(
                         out=acc[:, a, :],
-                        lhsT=codes[:, a * P : (a + 1) * P].bitcast(FP8X4),
-                        lhsT_scale=x_plane[:, a * P : (a + 1) * P],
-                        rhs=w_words[:, 2 * first_col : 2 * (first_col + cols)].bitcast(FP4X4),
-                        rhs_scale=w_plane[:, first_col : first_col + cols],
+                        lhsT=codes[:, tokens].bitcast(FP8X4),
+                        lhsT_scale=x_plane[:, tokens],
+                        rhs=w_words[:].bitcast(FP4X4),
+                        rhs_scale=w_plane[:],
                         start=True,
                         stop=True,
                     )
-            acc_tiles[r] = (q_acc, k_acc, v_acc)
+                banks.append(acc)
+            acc_tiles[r] = banks
 
         def rotate_and_store(r):
             b, first = batch_and_first_slot(r)
             slots = slice(first, first + ROUND_TILES)
-            q_acc, k_acc, v_acc = acc_tiles.pop(r)
-
+            shape = [P, BANK_TILES, ROPE_HEADS, PAIRS, 2]
+            from_even = work.tile([P, ROUND_TILES, ROPE_COLS], F32, name="from_even")
+            from_odd = work.tile([P, ROUND_TILES, ROPE_COLS], F32, name="from_odd")
+            q_sb = out_pool.tile([P, ROUND_TILES, Q_COLS], F32, name="q_sb")
+            k_sb = out_pool.tile([P, ROUND_TILES, LANES], F32, name="k_sb")
             v_sb = out_pool.tile([P, ROUND_TILES, LANES], F32, name="v_sb")
-            nc.scalar.copy(out=v_sb[:], in_=v_acc[:, :, LANES : 2 * LANES])
-            nc.sync.dma_start(out=v_view[b, :, slots, :], in_=v_sb[:])
-
-            for acc, heads, view, label in ((q_acc, Q_HEADS, q_view, "q"), (k_acc, 1, k_view, "k")):
-                shape = [P, ROUND_TILES, heads, PAIRS, 2]
-                pairs = acc[:, :, 0 : heads * LANES].rearrange(
-                    "p a (h i two) -> p a h i two", h=heads, two=2
+            banks = acc_tiles.pop(r)
+            for bank, acc in enumerate(banks):
+                tiles = slice(bank * BANK_TILES, (bank + 1) * BANK_TILES)
+                table_slots = slice(first + bank * BANK_TILES, first + (bank + 1) * BANK_TILES)
+                pairs = acc[:, :, 0:ROPE_COLS].rearrange(
+                    "p a (h i two) -> p a h i two", h=ROPE_HEADS, two=2
                 )
-                products = []
-                for lane, table in ((0, by_even), (1, by_odd)):
-                    product = work.tile(
-                        [P, ROUND_TILES, heads * LANES], F32, name="%s_product_%d" % (label, lane)
-                    )
+                for lane, table, product in ((0, by_even, from_even), (1, by_odd, from_odd)):
                     nc.vector.tensor_tensor(
-                        out=product[:].rearrange("p a (h i two) -> p a h i two", h=heads, two=2),
+                        out=product[:, tiles, :].rearrange(
+                            "p a (h i two) -> p a h i two", h=ROPE_HEADS, two=2
+                        ),
                         in0=pairs[:, :, :, :, lane : lane + 1].broadcast_to(shape),
-                        in1=table[:, slots, :]
+                        in1=table[:, table_slots, :]
                         .rearrange("p a (i two) -> p a i two", two=2)
                         .unsqueeze(2)
                         .broadcast_to(shape),
                         op=MULT,
                     )
-                    products.append(product)
-                rotated = out_pool.tile([P, ROUND_TILES, heads * LANES], F32, name="%s_sb" % label)
-                nc.gpsimd.tensor_tensor(
-                    out=rotated[:], in0=products[0][:], in1=products[1][:], op=ADD
-                )
-                nc.sync.dma_start(out=view[b, :, slots, :], in_=rotated[:])
+            q_adder = nc.vector if r == ROUNDS - 1 else nc.gpsimd
+            q_adder.tensor_tensor(
+                out=q_sb[:], in0=from_even[:, :, 0:Q_COLS], in1=from_odd[:, :, 0:Q_COLS], op=ADD
+            )
+            nc.gpsimd.tensor_tensor(
+                out=k_sb[:],
+                in0=from_even[:, :, Q_COLS:ROPE_COLS],
+                in1=from_odd[:, :, Q_COLS:ROPE_COLS],
+                op=ADD,
+            )
+            for bank, acc in enumerate(banks):
+                tiles = slice(bank * BANK_TILES, (bank + 1) * BANK_TILES)
+                nc.vector.tensor_copy(out=v_sb[:, tiles, :], in_=acc[:, :, ROPE_COLS:OUT_COLS])
+            nc.sync.dma_start(out=q_view[b, :, slots, :], in_=q_sb[:])
+            nc.sync.dma_start(out=k_view[b, :, slots, :], in_=k_sb[:])
+            nc.sync.dma_start(out=v_view[b, :, slots, :], in_=v_sb[:])
 
+        ctx.enter_context(tc.manual_schedule())
         for step in range(ROUNDS + 2):
             if step < ROUNDS:
                 transpose_and_regroup(step)
             if 1 <= step <= ROUNDS:
                 quantise(step - 1)
                 multiply(step - 1)
+            if step == 2:
+                build_tables()
             if step >= 2:
                 rotate_and_store(step - 2)

@@ -139,14 +139,11 @@ def tile_attention_pa_t_kernel(
             codes = work.tile([P, ROUND_TILES * P], U32, name="codes", align_bytes=64)
             x_plane = work.tile([P, ROUND_TILES * P], U8, name="x_plane", align_bytes=64)
             grouped = grouped_tiles.pop(r)
-            for bank in range(ROUND_BANKS):
-                tiles = slice(bank * BANK_TILES, (bank + 1) * BANK_TILES)
-                tokens = slice(bank * BANK_TILES * P, (bank + 1) * BANK_TILES * P)
-                nc.vector.quantize_mx(
-                    out=codes[:, tokens].bitcast(FP8X4),
-                    scales=x_plane[:, tokens],
-                    in_=grouped[:, tiles, :, :].rearrange("p a r j -> p (a r j)"),
-                )
+            nc.vector.quantize_mx(
+                out=codes[:].bitcast(FP8X4),
+                scales=x_plane[:],
+                in_=grouped[:].rearrange("p a r j -> p (a r j)"),
+            )
             code_tiles[r] = (codes, x_plane)
 
         def multiply(r):
@@ -180,6 +177,10 @@ def tile_attention_pa_t_kernel(
             banks = acc_tiles.pop(r)
             for bank, acc in enumerate(banks):
                 tiles = slice(bank * BANK_TILES, (bank + 1) * BANK_TILES)
+                nc.vector.tensor_copy(out=v_sb[:, tiles, :], in_=acc[:, :, ROPE_COLS:OUT_COLS])
+            nc.sync.dma_start(out=v_view[b, :, slots, :], in_=v_sb[:])
+            for bank, acc in enumerate(banks):
+                tiles = slice(bank * BANK_TILES, (bank + 1) * BANK_TILES)
                 table_slots = slice(first + bank * BANK_TILES, first + (bank + 1) * BANK_TILES)
                 pairs = acc[:, :, 0:ROPE_COLS].rearrange(
                     "p a (h i two) -> p a h i two", h=ROPE_HEADS, two=2
@@ -206,21 +207,17 @@ def tile_attention_pa_t_kernel(
                 in1=from_odd[:, :, Q_COLS:ROPE_COLS],
                 op=ADD,
             )
-            for bank, acc in enumerate(banks):
-                tiles = slice(bank * BANK_TILES, (bank + 1) * BANK_TILES)
-                nc.vector.tensor_copy(out=v_sb[:, tiles, :], in_=acc[:, :, ROPE_COLS:OUT_COLS])
             nc.sync.dma_start(out=q_view[b, :, slots, :], in_=q_sb[:])
             nc.sync.dma_start(out=k_view[b, :, slots, :], in_=k_sb[:])
-            nc.sync.dma_start(out=v_view[b, :, slots, :], in_=v_sb[:])
 
         ctx.enter_context(tc.manual_schedule())
-        for step in range(ROUNDS + 2):
+        for step in range(ROUNDS + 3):
             if step < ROUNDS:
                 transpose_and_regroup(step)
+            if step == 3:
+                build_tables()
+            if step >= 3:
+                rotate_and_store(step - 3)
             if 1 <= step <= ROUNDS:
                 quantise(step - 1)
                 multiply(step - 1)
-            if step == 2:
-                build_tables()
-            if step >= 2:
-                rotate_and_store(step - 2)

@@ -165,6 +165,15 @@ def tile_attention_pa_t_kernel(
                 banks.append(acc)
             acc_tiles[r] = banks
 
+        def copy_and_store_v(r):
+            b, first = batch_and_first_slot(r)
+            slots = slice(first, first + ROUND_TILES)
+            v_sb = out_pool.tile([P, ROUND_TILES, LANES], F32, name="v_sb")
+            for bank, acc in enumerate(acc_tiles[r]):
+                tiles = slice(bank * BANK_TILES, (bank + 1) * BANK_TILES)
+                nc.scalar.copy(out=v_sb[:, tiles, :], in_=acc[:, :, ROPE_COLS:OUT_COLS])
+            nc.sync.dma_start(out=v_view[b, :, slots, :], in_=v_sb[:])
+
         def rotate_and_store(r):
             b, first = batch_and_first_slot(r)
             slots = slice(first, first + ROUND_TILES)
@@ -173,12 +182,7 @@ def tile_attention_pa_t_kernel(
             from_odd = work.tile([P, ROUND_TILES, ROPE_COLS], F32, name="from_odd")
             q_sb = out_pool.tile([P, ROUND_TILES, Q_COLS], F32, name="q_sb")
             k_sb = out_pool.tile([P, ROUND_TILES, LANES], F32, name="k_sb")
-            v_sb = out_pool.tile([P, ROUND_TILES, LANES], F32, name="v_sb")
             banks = acc_tiles.pop(r)
-            for bank, acc in enumerate(banks):
-                tiles = slice(bank * BANK_TILES, (bank + 1) * BANK_TILES)
-                nc.vector.tensor_copy(out=v_sb[:, tiles, :], in_=acc[:, :, ROPE_COLS:OUT_COLS])
-            nc.sync.dma_start(out=v_view[b, :, slots, :], in_=v_sb[:])
             for bank, acc in enumerate(banks):
                 tiles = slice(bank * BANK_TILES, (bank + 1) * BANK_TILES)
                 table_slots = slice(first + bank * BANK_TILES, first + (bank + 1) * BANK_TILES)
@@ -212,6 +216,8 @@ def tile_attention_pa_t_kernel(
 
         ctx.enter_context(tc.manual_schedule())
         for step in range(ROUNDS + 3):
+            if step >= 3:
+                copy_and_store_v(step - 3)
             if step < ROUNDS:
                 transpose_and_regroup(step)
             if step == 3:

@@ -216,8 +216,8 @@ def tile_attention_pa_t_kernel(
 
         ctx.enter_context(tc.manual_schedule())
         for step in range(ROUNDS + 3):
-            if step >= 3:
-                copy_and_store_v(step - 3)
+            if 2 <= step <= ROUNDS + 1:
+                copy_and_store_v(step - 2)
             if step < ROUNDS:
                 transpose_and_regroup(step)
             if step == 3:

@@ -30,6 +30,7 @@ BANK_TILES = 2
 ROUND_BANKS = ROUND_TILES // BANK_TILES
 ROUNDS_PER_BATCH = SLOTS // ROUND_TILES
 ROUNDS = BATCH * ROUNDS_PER_BATCH
+VECTOR_ADDS = 2
 
 FLOPS = 2 * BATCH * SEQ * HIDDEN * OUT_COLS
 
@@ -84,8 +85,6 @@ def tile_attention_pa_t_kernel(
                 in_=w_qkv_scales[0, 4 * quadrant : 4 * quadrant + 4, :].bitcast(I32),
             )
 
-        by_even = const.tile([P, SLOTS, LANES], BF16)
-        by_odd = const.tile([P, SLOTS, LANES], BF16)
         cos_sb = const.tile([P, SLOTS, LANES], BF16)
         sin_sb = const.tile([P, SLOTS, LANES], BF16)
         nc.sync.dma_start(out=sin_sb[:], in_=sin_view)
@@ -94,17 +93,10 @@ def tile_attention_pa_t_kernel(
             for bank in range(ROUND_BANKS):
                 load_x(r, bank)
 
-        def lanes(table, lane):
-            return table[:].rearrange("p t (i two) -> p t i two", two=2)[:, :, :, lane]
-
         def build_tables():
-            nc.vector.tensor_copy(out=lanes(by_even, 1), in_=lanes(sin_sb, 1))
-            nc.vector.tensor_copy(out=lanes(by_even, 0), in_=lanes(cos_sb, 0))
+            even_lanes = sin_sb[:].rearrange("p t (i two) -> p t i two", two=2)[:, :, :, 0]
             nc.gpsimd.tensor_scalar(
-                out=lanes(by_odd, 0), in0=lanes(sin_sb, 0), scalar1=-1.0, scalar2=0.0, op0=MULT, op1=ADD
-            )
-            nc.gpsimd.tensor_scalar(
-                out=lanes(by_odd, 1), in0=lanes(cos_sb, 1), scalar1=1.0, scalar2=0.0, op0=MULT, op1=ADD
+                out=even_lanes, in0=even_lanes, scalar1=-1.0, scalar2=0.0, op0=MULT, op1=ADD
             )
 
         grouped_tiles = {}
@@ -174,14 +166,14 @@ def tile_attention_pa_t_kernel(
                 nc.scalar.copy(out=v_sb[:, tiles, :], in_=acc[:, :, ROPE_COLS:OUT_COLS])
             nc.sync.dma_start(out=v_view[b, :, slots, :], in_=v_sb[:])
 
-        def rotate_and_store(r):
-            b, first = batch_and_first_slot(r)
-            slots = slice(first, first + ROUND_TILES)
+        product_tiles = {}
+
+        def multiply_by_tables(r):
+            first = batch_and_first_slot(r)[1]
             shape = [P, BANK_TILES, ROPE_HEADS, PAIRS, 2]
             from_even = work.tile([P, ROUND_TILES, ROPE_COLS], F32, name="from_even")
             from_odd = work.tile([P, ROUND_TILES, ROPE_COLS], F32, name="from_odd")
-            q_sb = out_pool.tile([P, ROUND_TILES, Q_COLS], F32, name="q_sb")
-            k_sb = out_pool.tile([P, ROUND_TILES, LANES], F32, name="k_sb")
+            product_tiles[r] = (from_even, from_odd)
             banks = acc_tiles.pop(r)
             for bank, acc in enumerate(banks):
                 tiles = slice(bank * BANK_TILES, (bank + 1) * BANK_TILES)
@@ -189,29 +181,38 @@ def tile_attention_pa_t_kernel(
                 pairs = acc[:, :, 0:ROPE_COLS].rearrange(
                     "p a (h i two) -> p a h i two", h=ROPE_HEADS, two=2
                 )
-                for lane, table, product in ((0, by_even, from_even), (1, by_odd, from_odd)):
+                for operand, table, product in (
+                    (pairs, cos_sb, from_even),
+                    (pairs[:, :, :, :, ::-1], sin_sb, from_odd),
+                ):
                     nc.vector.tensor_tensor(
                         out=product[:, tiles, :].rearrange(
                             "p a (h i two) -> p a h i two", h=ROPE_HEADS, two=2
                         ),
-                        in0=pairs[:, :, :, :, lane : lane + 1].broadcast_to(shape),
+                        in0=operand,
                         in1=table[:, table_slots, :]
                         .rearrange("p a (i two) -> p a i two", two=2)
                         .unsqueeze(2)
                         .broadcast_to(shape),
                         op=MULT,
                     )
-            q_adder = nc.vector if r == ROUNDS - 1 else nc.gpsimd
-            q_adder.tensor_tensor(
+
+        def add_and_store(r, engine):
+            b, first = batch_and_first_slot(r)
+            slots = slice(first, first + ROUND_TILES)
+            from_even, from_odd = product_tiles.pop(r)
+            q_sb = out_pool.tile([P, ROUND_TILES, Q_COLS], F32, name="q_sb")
+            k_sb = out_pool.tile([P, ROUND_TILES, LANES], F32, name="k_sb")
+            engine.tensor_tensor(
                 out=q_sb[:], in0=from_even[:, :, 0:Q_COLS], in1=from_odd[:, :, 0:Q_COLS], op=ADD
             )
-            nc.gpsimd.tensor_tensor(
+            nc.sync.dma_start(out=q_view[b, :, slots, :], in_=q_sb[:])
+            engine.tensor_tensor(
                 out=k_sb[:],
                 in0=from_even[:, :, Q_COLS:ROPE_COLS],
                 in1=from_odd[:, :, Q_COLS:ROPE_COLS],
                 op=ADD,
             )
-            nc.sync.dma_start(out=q_view[b, :, slots, :], in_=q_sb[:])
             nc.sync.dma_start(out=k_view[b, :, slots, :], in_=k_sb[:])
 
         ctx.enter_context(tc.manual_schedule())
@@ -223,7 +224,11 @@ def tile_attention_pa_t_kernel(
             if step == 3:
                 build_tables()
             if step >= 3:
-                rotate_and_store(step - 3)
+                multiply_by_tables(step - 3)
+            if 3 <= step < ROUNDS + 3 - VECTOR_ADDS:
+                add_and_store(step - 3, nc.gpsimd)
             if 1 <= step <= ROUNDS:
                 quantise(step - 1)
                 multiply(step - 1)
+        for r in range(ROUNDS - VECTOR_ADDS, ROUNDS):
+            add_and_store(r, nc.vector)

@@ -31,6 +31,9 @@ ROUND_BANKS = ROUND_TILES // BANK_TILES
 ROUNDS_PER_BATCH = SLOTS // ROUND_TILES
 ROUNDS = BATCH * ROUNDS_PER_BATCH
 VECTOR_ADDS = 2
+SPAN_ROUNDS = 2
+SPAN_TILES = SPAN_ROUNDS * ROUND_TILES
+SPANS = ROUNDS // SPAN_ROUNDS
 
 FLOPS = 2 * BATCH * SEQ * HIDDEN * OUT_COLS
 
@@ -49,8 +52,8 @@ def tile_attention_pa_t_kernel(
 
     with ExitStack() as ctx:
         const = ctx.enter_context(tc.tile_pool(name="const", bufs=1))
-        x_pool = ctx.enter_context(tc.tile_pool(name="x", bufs=ROUNDS))
-        out_pool = ctx.enter_context(tc.tile_pool(name="out", bufs=ROUNDS))
+        x_pool = ctx.enter_context(tc.tile_pool(name="x", bufs=SPANS))
+        out_pool = ctx.enter_context(tc.tile_pool(name="out", bufs=SPANS))
         work = ctx.enter_context(tc.tile_pool(name="work", bufs=3))
         xt_pool = ctx.enter_context(tc.psum_pool(name="xt", bufs=2 * ROUND_BANKS))
         acc_pool = ctx.enter_context(tc.psum_pool(name="acc", bufs=2 * ROUND_BANKS))
@@ -58,25 +61,48 @@ def tile_attention_pa_t_kernel(
         def batch_and_first_slot(r):
             return r // ROUNDS_PER_BATCH, (r % ROUNDS_PER_BATCH) * ROUND_TILES
 
-        x_tiles = []
+        def tiles_in_span(r):
+            return slice((r % SPAN_ROUNDS) * ROUND_TILES, (r % SPAN_ROUNDS + 1) * ROUND_TILES)
 
-        def load_x(r, bank):
+        x_spans = []
+
+        def load_x(span, pieces):
+            b, first = batch_and_first_slot(span * SPAN_ROUNDS)
+            x_sb = x_pool.tile([P, SPAN_TILES, HIDDEN], BF16, name="x_sb")
+            x_spans.append(x_sb)
+            t = 0
+            for tiles in pieces:
+                nc.sync.dma_start(
+                    out=x_sb[:, t : t + tiles, :], in_=x_view[b, :, first + t : first + t + tiles, :]
+                )
+                t += tiles
+
+        out_spans = {}
+
+        def out_tile(name, cols, r):
+            if r % SPAN_ROUNDS == 0:
+                out_spans[name] = out_pool.tile([P, SPAN_TILES, cols], F32, name=name)
+            return out_spans[name][:, tiles_in_span(r), :]
+
+        def store(name, view, r):
             b, first = batch_and_first_slot(r)
-            if bank == 0:
-                x_sb = x_pool.tile([P, ROUND_TILES, HIDDEN], BF16, name="x_sb")
-                x_tiles.append(x_sb)
-            tiles = slice(bank * BANK_TILES, (bank + 1) * BANK_TILES)
-            slots = slice(first + bank * BANK_TILES, first + (bank + 1) * BANK_TILES)
-            nc.sync.dma_start(out=x_tiles[r][:, tiles, :], in_=x_view[b, :, slots, :])
+            if r >= ROUNDS - SPAN_ROUNDS:
+                nc.sync.dma_start(
+                    out=view[b, :, first : first + ROUND_TILES, :],
+                    in_=out_spans[name][:, tiles_in_span(r), :],
+                )
+            elif r % SPAN_ROUNDS == SPAN_ROUNDS - 1:
+                nc.sync.dma_start(
+                    out=view[b, :, first + ROUND_TILES - SPAN_TILES : first + ROUND_TILES, :],
+                    in_=out_spans[name][:],
+                )
 
         w_plane = const.tile([P, OUT_COLS], U8, align_bytes=64)
         nc.vector.memset(w_plane[:].bitcast(I32), 0)
         ident = const.tile([P, P], F32)
         make_identity(nc, ident[:])
 
-        for r in range(2):
-            for bank in range(ROUND_BANKS):
-                load_x(r, bank)
+        load_x(0, (BANK_TILES,) * (SPAN_TILES // BANK_TILES))
         w_words = const.tile([P, 2 * OUT_COLS], U8, align_bytes=64)
         nc.sync.dma_start(out=w_words[:].bitcast(I32), in_=w_qkv_words[0].bitcast(I32))
         for quadrant in range(4):
@@ -89,9 +115,9 @@ def tile_attention_pa_t_kernel(
         sin_sb = const.tile([P, SLOTS, LANES], BF16)
         nc.sync.dma_start(out=sin_sb[:], in_=sin_view)
         nc.sync.dma_start(out=cos_sb[:], in_=cos_view)
-        for r in range(2, ROUNDS):
-            for bank in range(ROUND_BANKS):
-                load_x(r, bank)
+        load_x(1, (BANK_TILES, BANK_TILES, ROUND_TILES))
+        for span in range(2, SPANS):
+            load_x(span, (SPAN_TILES,))
 
         def build_tables():
             even_lanes = sin_sb[:].rearrange("p t (i two) -> p t i two", two=2)[:, :, :, 0]
@@ -104,7 +130,7 @@ def tile_attention_pa_t_kernel(
         acc_tiles = {}
 
         def transpose_and_regroup(r):
-            x_words = x_tiles[r][:].bitcast(F32)
+            x_words = x_spans[r // SPAN_ROUNDS][:, tiles_in_span(r), :].bitcast(F32)
             grouped = work.tile([P, ROUND_TILES, P, 4], BF16, name="grouped", align_bytes=64)
             grouped_words = (
                 grouped[:]
@@ -158,13 +184,11 @@ def tile_attention_pa_t_kernel(
             acc_tiles[r] = banks
 
         def copy_and_store_v(r):
-            b, first = batch_and_first_slot(r)
-            slots = slice(first, first + ROUND_TILES)
-            v_sb = out_pool.tile([P, ROUND_TILES, LANES], F32, name="v_sb")
+            v_sb = out_tile("v_sb", LANES, r)
             for bank, acc in enumerate(acc_tiles[r]):
                 tiles = slice(bank * BANK_TILES, (bank + 1) * BANK_TILES)
                 nc.scalar.copy(out=v_sb[:, tiles, :], in_=acc[:, :, ROPE_COLS:OUT_COLS])
-            nc.sync.dma_start(out=v_view[b, :, slots, :], in_=v_sb[:])
+            store("v_sb", v_view, r)
 
         product_tiles = {}
 
@@ -198,22 +222,21 @@ def tile_attention_pa_t_kernel(
                     )
 
         def add_and_store(r, engine):
-            b, first = batch_and_first_slot(r)
-            slots = slice(first, first + ROUND_TILES)
             from_even, from_odd = product_tiles.pop(r)
-            q_sb = out_pool.tile([P, ROUND_TILES, Q_COLS], F32, name="q_sb")
-            k_sb = out_pool.tile([P, ROUND_TILES, LANES], F32, name="k_sb")
             engine.tensor_tensor(
-                out=q_sb[:], in0=from_even[:, :, 0:Q_COLS], in1=from_odd[:, :, 0:Q_COLS], op=ADD
+                out=out_tile("q_sb", Q_COLS, r),
+                in0=from_even[:, :, 0:Q_COLS],
+                in1=from_odd[:, :, 0:Q_COLS],
+                op=ADD,
             )
-            nc.sync.dma_start(out=q_view[b, :, slots, :], in_=q_sb[:])
+            store("q_sb", q_view, r)
             engine.tensor_tensor(
-                out=k_sb[:],
+                out=out_tile("k_sb", LANES, r),
                 in0=from_even[:, :, Q_COLS:ROPE_COLS],
                 in1=from_odd[:, :, Q_COLS:ROPE_COLS],
                 op=ADD,
             )
-            nc.sync.dma_start(out=k_view[b, :, slots, :], in_=k_sb[:])
+            store("k_sb", k_view, r)
 
         ctx.enter_context(tc.manual_schedule())
         for step in range(ROUNDS + 3):

@@ -84,17 +84,17 @@ def tile_attention_pa_t_kernel(
                 out_spans[name] = out_pool.tile([P, SPAN_TILES, cols], F32, name=name)
             return out_spans[name][:, tiles_in_span(r), :]
 
-        def store(name, view, r):
+        def store(name, view, r, cols):
             b, first = batch_and_first_slot(r)
             if r >= ROUNDS - SPAN_ROUNDS:
                 nc.sync.dma_start(
                     out=view[b, :, first : first + ROUND_TILES, :],
-                    in_=out_spans[name][:, tiles_in_span(r), :],
+                    in_=out_spans[name][:, tiles_in_span(r), cols],
                 )
             elif r % SPAN_ROUNDS == SPAN_ROUNDS - 1:
                 nc.sync.dma_start(
                     out=view[b, :, first + ROUND_TILES - SPAN_TILES : first + ROUND_TILES, :],
-                    in_=out_spans[name][:],
+                    in_=out_spans[name][:, :, cols],
                 )
 
         w_plane = const.tile([P, OUT_COLS], U8, align_bytes=64)
@@ -188,7 +188,7 @@ def tile_attention_pa_t_kernel(
             for bank, acc in enumerate(acc_tiles[r]):
                 tiles = slice(bank * BANK_TILES, (bank + 1) * BANK_TILES)
                 nc.scalar.copy(out=v_sb[:, tiles, :], in_=acc[:, :, ROPE_COLS:OUT_COLS])
-            store("v_sb", v_view, r)
+            store("v_sb", v_view, r, slice(0, LANES))
 
         product_tiles = {}
 
@@ -221,22 +221,24 @@ def tile_attention_pa_t_kernel(
                         op=MULT,
                     )
 
-        def add_and_store(r, engine):
+        def add_and_store(r, engine, together):
             from_even, from_odd = product_tiles.pop(r)
-            engine.tensor_tensor(
-                out=out_tile("q_sb", Q_COLS, r),
-                in0=from_even[:, :, 0:Q_COLS],
-                in1=from_odd[:, :, 0:Q_COLS],
-                op=ADD,
-            )
-            store("q_sb", q_view, r)
-            engine.tensor_tensor(
-                out=out_tile("k_sb", LANES, r),
-                in0=from_even[:, :, Q_COLS:ROPE_COLS],
-                in1=from_odd[:, :, Q_COLS:ROPE_COLS],
-                op=ADD,
-            )
-            store("k_sb", k_view, r)
+            if together:
+                engine.tensor_tensor(
+                    out=out_tile("qk_sb", ROPE_COLS, r), in0=from_even[:], in1=from_odd[:], op=ADD
+                )
+                store("qk_sb", q_view, r, slice(0, Q_COLS))
+                store("qk_sb", k_view, r, slice(Q_COLS, ROPE_COLS))
+            else:
+                for name, view, cols in (
+                    ("q_sb", q_view, slice(0, Q_COLS)),
+                    ("k_sb", k_view, slice(Q_COLS, ROPE_COLS)),
+                ):
+                    width = cols.stop - cols.start
+                    engine.tensor_tensor(
+                        out=out_tile(name, width, r), in0=from_even[:, :, cols], in1=from_odd[:, :, cols], op=ADD
+                    )
+                    store(name, view, r, slice(0, width))
 
         ctx.enter_context(tc.manual_schedule())
         for step in range(ROUNDS + 3):
@@ -249,9 +251,9 @@ def tile_attention_pa_t_kernel(
             if step >= 3:
                 multiply_by_tables(step - 3)
             if 3 <= step < ROUNDS + 3 - VECTOR_ADDS:
-                add_and_store(step - 3, nc.gpsimd)
+                add_and_store(step - 3, nc.gpsimd, True)
             if 1 <= step <= ROUNDS:
                 quantise(step - 1)
                 multiply(step - 1)
         for r in range(ROUNDS - VECTOR_ADDS, ROUNDS):
-            add_and_store(r, nc.vector)
+            add_and_store(r, nc.vector, False)

@@ -30,7 +30,8 @@ BANK_TILES = 2
 ROUND_BANKS = ROUND_TILES // BANK_TILES
 ROUNDS_PER_BATCH = SLOTS // ROUND_TILES
 ROUNDS = BATCH * ROUNDS_PER_BATCH
-VECTOR_ADDS = 2
+VECTOR_ADDS = 1
+LONG_RUN_ROUNDS = 2
 SPAN_ROUNDS = 2
 SPAN_TILES = SPAN_ROUNDS * ROUND_TILES
 SPANS = ROUNDS // SPAN_ROUNDS
@@ -53,7 +54,7 @@ def tile_attention_pa_t_kernel(
     with ExitStack() as ctx:
         const = ctx.enter_context(tc.tile_pool(name="const", bufs=1))
         x_pool = ctx.enter_context(tc.tile_pool(name="x", bufs=SPANS))
-        out_pool = ctx.enter_context(tc.tile_pool(name="out", bufs=SPANS))
+        out_pool = ctx.enter_context(tc.tile_pool(name="out", bufs=ROUNDS))
         work = ctx.enter_context(tc.tile_pool(name="work", bufs=3))
         xt_pool = ctx.enter_context(tc.psum_pool(name="xt", bufs=2 * ROUND_BANKS))
         acc_pool = ctx.enter_context(tc.psum_pool(name="acc", bufs=2 * ROUND_BANKS))
@@ -77,25 +78,9 @@ def tile_attention_pa_t_kernel(
                 )
                 t += tiles
 
-        out_spans = {}
-
-        def out_tile(name, cols, r):
-            if r % SPAN_ROUNDS == 0:
-                out_spans[name] = out_pool.tile([P, SPAN_TILES, cols], F32, name=name)
-            return out_spans[name][:, tiles_in_span(r), :]
-
-        def store(name, view, r, cols):
+        def store(tile, view, r, cols):
             b, first = batch_and_first_slot(r)
-            if r >= ROUNDS - SPAN_ROUNDS:
-                nc.sync.dma_start(
-                    out=view[b, :, first : first + ROUND_TILES, :],
-                    in_=out_spans[name][:, tiles_in_span(r), cols],
-                )
-            elif r % SPAN_ROUNDS == SPAN_ROUNDS - 1:
-                nc.sync.dma_start(
-                    out=view[b, :, first + ROUND_TILES - SPAN_TILES : first + ROUND_TILES, :],
-                    in_=out_spans[name][:, :, cols],
-                )
+            nc.sync.dma_start(out=view[b, :, first : first + ROUND_TILES, :], in_=tile[:, :, cols])
 
         w_plane = const.tile([P, OUT_COLS], U8, align_bytes=64)
         nc.vector.memset(w_plane[:].bitcast(I32), 0)
@@ -184,11 +169,11 @@ def tile_attention_pa_t_kernel(
             acc_tiles[r] = banks
 
         def copy_and_store_v(r):
-            v_sb = out_tile("v_sb", LANES, r)
+            v_sb = out_pool.tile([P, ROUND_TILES, LANES], F32, name="v_sb")
             for bank, acc in enumerate(acc_tiles[r]):
                 tiles = slice(bank * BANK_TILES, (bank + 1) * BANK_TILES)
                 nc.scalar.copy(out=v_sb[:, tiles, :], in_=acc[:, :, ROPE_COLS:OUT_COLS])
-            store("v_sb", v_view, r, slice(0, LANES))
+            store(v_sb, v_view, r, slice(0, LANES))
 
         product_tiles = {}
 
@@ -224,21 +209,21 @@ def tile_attention_pa_t_kernel(
         def add_and_store(r, engine, together):
             from_even, from_odd = product_tiles.pop(r)
             if together:
-                engine.tensor_tensor(
-                    out=out_tile("qk_sb", ROPE_COLS, r), in0=from_even[:], in1=from_odd[:], op=ADD
-                )
-                store("qk_sb", q_view, r, slice(0, Q_COLS))
-                store("qk_sb", k_view, r, slice(Q_COLS, ROPE_COLS))
+                qk_sb = out_pool.tile([P, ROUND_TILES, ROPE_COLS], F32, name="qk_sb")
+                engine.tensor_tensor(out=qk_sb[:], in0=from_even[:], in1=from_odd[:], op=ADD)
+                store(qk_sb, q_view, r, slice(0, Q_COLS))
+                store(qk_sb, k_view, r, slice(Q_COLS, ROPE_COLS))
             else:
                 for name, view, cols in (
                     ("q_sb", q_view, slice(0, Q_COLS)),
                     ("k_sb", k_view, slice(Q_COLS, ROPE_COLS)),
                 ):
                     width = cols.stop - cols.start
+                    out_sb = out_pool.tile([P, ROUND_TILES, width], F32, name=name, bufs=LONG_RUN_ROUNDS)
                     engine.tensor_tensor(
-                        out=out_tile(name, width, r), in0=from_even[:, :, cols], in1=from_odd[:, :, cols], op=ADD
+                        out=out_sb[:], in0=from_even[:, :, cols], in1=from_odd[:, :, cols], op=ADD
                     )
-                    store(name, view, r, slice(0, width))
+                    store(out_sb, view, r, slice(0, width))
 
         ctx.enter_context(tc.manual_schedule())
         for step in range(ROUNDS + 3):
@@ -251,7 +236,7 @@ def tile_attention_pa_t_kernel(
             if step >= 3:
                 multiply_by_tables(step - 3)
             if 3 <= step < ROUNDS + 3 - VECTOR_ADDS:
-                add_and_store(step - 3, nc.gpsimd, True)
+                add_and_store(step - 3, nc.gpsimd, step - 3 < ROUNDS - LONG_RUN_ROUNDS)
             if 1 <= step <= ROUNDS:
                 quantise(step - 1)
                 multiply(step - 1)

@@ -168,12 +168,34 @@ def tile_attention_pa_t_kernel(
                 banks.append(acc)
             acc_tiles[r] = banks
 
+        span_tiles = {}
+
+        def span_tile(name, r):
+            key = (name, r // SPAN_ROUNDS)
+            if key not in span_tiles:
+                span_tiles[key] = out_pool.tile([P, SPAN_TILES, LANES], F32, name=name, bufs=SPANS)
+            return span_tiles[key]
+
+        def store_span(name, view, r):
+            if r % SPAN_ROUNDS == SPAN_ROUNDS - 1:
+                b, first = batch_and_first_slot(r - r % SPAN_ROUNDS)
+                nc.sync.dma_start(
+                    out=view[b, :, first : first + SPAN_TILES, :], in_=span_tiles.pop((name, r // SPAN_ROUNDS))[:]
+                )
+
         def copy_and_store_v(r):
-            v_sb = out_pool.tile([P, ROUND_TILES, LANES], F32, name="v_sb")
+            v_sb = span_tile("v_sb", r)
             for bank, acc in enumerate(acc_tiles[r]):
-                tiles = slice(bank * BANK_TILES, (bank + 1) * BANK_TILES)
-                nc.scalar.copy(out=v_sb[:, tiles, :], in_=acc[:, :, ROPE_COLS:OUT_COLS])
-            store(v_sb, v_view, r, slice(0, LANES))
+                t = (r % SPAN_ROUNDS) * ROUND_TILES + bank * BANK_TILES
+                nc.scalar.copy(out=v_sb[:, t : t + BANK_TILES, :], in_=acc[:, :, ROPE_COLS:OUT_COLS])
+            store_span("v_sb", v_view, r)
+
+        joint_tiles = {}
+
+        def gather_and_store_k(r):
+            k_sb = span_tile("k_span", r)
+            nc.scalar.copy(out=k_sb[:, tiles_in_span(r), :], in_=joint_tiles.pop(r)[:, :, Q_COLS:ROPE_COLS])
+            store_span("k_span", k_view, r)
 
         product_tiles = {}
 
@@ -212,7 +234,7 @@ def tile_attention_pa_t_kernel(
                 qk_sb = out_pool.tile([P, ROUND_TILES, ROPE_COLS], F32, name="qk_sb")
                 engine.tensor_tensor(out=qk_sb[:], in0=from_even[:], in1=from_odd[:], op=ADD)
                 store(qk_sb, q_view, r, slice(0, Q_COLS))
-                store(qk_sb, k_view, r, slice(Q_COLS, ROPE_COLS))
+                joint_tiles[r] = qk_sb
             else:
                 for name, view, cols in (
                     ("q_sb", q_view, slice(0, Q_COLS)),
@@ -229,6 +251,8 @@ def tile_attention_pa_t_kernel(
         for step in range(ROUNDS + 3):
             if 2 <= step <= ROUNDS + 1:
                 copy_and_store_v(step - 2)
+            if 0 <= step - 5 < ROUNDS - LONG_RUN_ROUNDS:
+                gather_and_store_k(step - 5)
             if step < ROUNDS:
                 transpose_and_regroup(step)
             if step == 3:

@@ -32,6 +32,7 @@ ROUNDS_PER_BATCH = SLOTS // ROUND_TILES
 ROUNDS = BATCH * ROUNDS_PER_BATCH
 VECTOR_ADDS = 1
 LONG_RUN_ROUNDS = 2
+LATE_ROUNDS = 4
 SPAN_ROUNDS = 2
 SPAN_TILES = SPAN_ROUNDS * ROUND_TILES
 SPANS = ROUNDS // SPAN_ROUNDS
@@ -184,11 +185,20 @@ def tile_attention_pa_t_kernel(
                 )
 
         def copy_and_store_v(r):
-            v_sb = span_tile("v_sb", r)
+            by_span = r < ROUNDS - LONG_RUN_ROUNDS
+            if by_span:
+                v_sb = span_tile("v_sb", r)
+                first_tile = (r % SPAN_ROUNDS) * ROUND_TILES
+            else:
+                v_sb = out_pool.tile([P, ROUND_TILES, LANES], F32, name="v_late", bufs=LONG_RUN_ROUNDS)
+                first_tile = 0
             for bank, acc in enumerate(acc_tiles[r]):
-                t = (r % SPAN_ROUNDS) * ROUND_TILES + bank * BANK_TILES
+                t = first_tile + bank * BANK_TILES
                 nc.scalar.copy(out=v_sb[:, t : t + BANK_TILES, :], in_=acc[:, :, ROPE_COLS:OUT_COLS])
-            store_span("v_sb", v_view, r)
+            if by_span:
+                store_span("v_sb", v_view, r)
+            else:
+                store(v_sb, v_view, r, slice(0, LANES))
 
         joint_tiles = {}
 
@@ -234,7 +244,10 @@ def tile_attention_pa_t_kernel(
                 qk_sb = out_pool.tile([P, ROUND_TILES, ROPE_COLS], F32, name="qk_sb")
                 engine.tensor_tensor(out=qk_sb[:], in0=from_even[:], in1=from_odd[:], op=ADD)
                 store(qk_sb, q_view, r, slice(0, Q_COLS))
-                joint_tiles[r] = qk_sb
+                if r < ROUNDS - LATE_ROUNDS:
+                    joint_tiles[r] = qk_sb
+                else:
+                    store(qk_sb, k_view, r, slice(Q_COLS, ROPE_COLS))
             else:
                 for name, view, cols in (
                     ("q_sb", q_view, slice(0, Q_COLS)),
@@ -251,7 +264,7 @@ def tile_attention_pa_t_kernel(
         for step in range(ROUNDS + 3):
             if 2 <= step <= ROUNDS + 1:
                 copy_and_store_v(step - 2)
-            if 0 <= step - 5 < ROUNDS - LONG_RUN_ROUNDS:
+            if 0 <= step - 5 < ROUNDS - LATE_ROUNDS:
                 gather_and_store_k(step - 5)
             if step < ROUNDS:
                 transpose_and_regroup(step)

@@ -68,12 +68,19 @@ def tile_attention_pa_t_kernel(
 
         x_spans = []
 
-        def load_x(span, pieces):
+        def load_x(span, pieces, table_slots=(), more_pieces=()):
             b, first = batch_and_first_slot(span * SPAN_ROUNDS)
             x_sb = x_pool.tile([P, SPAN_TILES, HIDDEN], BF16, name="x_sb")
             x_spans.append(x_sb)
             t = 0
             for tiles in pieces:
+                nc.sync.dma_start(
+                    out=x_sb[:, t : t + tiles, :], in_=x_view[b, :, first + t : first + t + tiles, :]
+                )
+                t += tiles
+            for slots in table_slots:
+                load_tables(slots)
+            for tiles in more_pieces:
                 nc.sync.dma_start(
                     out=x_sb[:, t : t + tiles, :], in_=x_view[b, :, first + t : first + t + tiles, :]
                 )
@@ -99,17 +106,22 @@ def tile_attention_pa_t_kernel(
 
         cos_sb = const.tile([P, SLOTS, LANES], BF16)
         sin_sb = const.tile([P, SLOTS, LANES], BF16)
-        nc.sync.dma_start(out=sin_sb[:], in_=sin_view)
-        nc.sync.dma_start(out=cos_sb[:], in_=cos_view)
-        load_x(1, (BANK_TILES, BANK_TILES, ROUND_TILES))
+
+        def load_tables(slots):
+            nc.sync.dma_start(out=sin_sb[:, slots, :], in_=sin_view[:, slots, :])
+            nc.sync.dma_start(out=cos_sb[:, slots, :], in_=cos_view[:, slots, :])
+
+        load_tables(slice(0, ROUND_TILES))
+        load_x(1, (BANK_TILES, BANK_TILES), (slice(ROUND_TILES, SLOTS),), (ROUND_TILES,))
         for span in range(2, SPANS):
             load_x(span, (SPAN_TILES,))
 
         def build_tables():
-            even_lanes = sin_sb[:].rearrange("p t (i two) -> p t i two", two=2)[:, :, :, 0]
-            nc.gpsimd.tensor_scalar(
-                out=even_lanes, in0=even_lanes, scalar1=-1.0, scalar2=0.0, op0=MULT, op1=ADD
-            )
+            for slots in (slice(0, ROUND_TILES), slice(ROUND_TILES, SLOTS)):
+                even_lanes = sin_sb[:, slots, :].rearrange("p t (i two) -> p t i two", two=2)[:, :, :, 0]
+                nc.gpsimd.tensor_scalar(
+                    out=even_lanes, in0=even_lanes, scalar1=-1.0, scalar2=0.0, op0=MULT, op1=ADD
+                )
 
         grouped_tiles = {}
         code_tiles = {}

from contextlib import ExitStack

import concourse.mybir as mybir
from concourse.masks import make_identity

BF16 = mybir.dt.bfloat16
F32 = mybir.dt.float32
I32 = mybir.dt.int32
U8 = mybir.dt.uint8
U32 = mybir.dt.uint32
FP8X4 = mybir.dt.float8_e4m3fn_x4
FP4X4 = mybir.dt.float4_e2m1fn_x4
MULT = mybir.AluOpType.mult
ADD = mybir.AluOpType.add

P = 128
BATCH = 4
SEQ = 2048
HIDDEN = 512
LANES = 64
ROPE_HEADS = 3
Q_COLS = 2 * LANES
ROPE_COLS = ROPE_HEADS * LANES
OUT_COLS = 4 * LANES
PAIRS = LANES // 2

SLOTS = SEQ // P
ROUND_TILES = 4
BANK_TILES = 2
ROUND_BANKS = ROUND_TILES // BANK_TILES
ROUNDS_PER_BATCH = SLOTS // ROUND_TILES
ROUNDS = BATCH * ROUNDS_PER_BATCH
VECTOR_ADDS = 1
LONG_RUN_ROUNDS = 2
LATE_ROUNDS = 4
SPAN_ROUNDS = 2
SPAN_TILES = SPAN_ROUNDS * ROUND_TILES
SPANS = ROUNDS // SPAN_ROUNDS

FLOPS = 2 * BATCH * SEQ * HIDDEN * OUT_COLS


def tile_attention_pa_t_kernel(
    tc, hidden_states, cos, sin, w_qkv_words, w_qkv_scales, out_0, out_1, out_2
):
    nc = tc.nc

    x_view = hidden_states.rearrange("b (p t) k -> b p t k", t=SLOTS)
    q_view = out_0.rearrange("b (p t) h d -> b p t (h d)", t=SLOTS)
    k_view = out_1.rearrange("b (p t) h d -> b p t (h d)", t=SLOTS)
    v_view = out_2.rearrange("b (p t) h d -> b p t (h d)", t=SLOTS)
    cos_view = cos.rearrange("(p t) d -> p t d", t=SLOTS)
    sin_view = sin.rearrange("(p t) d -> p t d", t=SLOTS)

    with ExitStack() as ctx:
        const = ctx.enter_context(tc.tile_pool(name="const", bufs=1))
        x_pool = ctx.enter_context(tc.tile_pool(name="x", bufs=SPANS))
        out_pool = ctx.enter_context(tc.tile_pool(name="out", bufs=ROUNDS))
        work = ctx.enter_context(tc.tile_pool(name="work", bufs=3))
        xt_pool = ctx.enter_context(tc.psum_pool(name="xt", bufs=2 * ROUND_BANKS))
        acc_pool = ctx.enter_context(tc.psum_pool(name="acc", bufs=2 * ROUND_BANKS))

        def batch_and_first_slot(r):
            return r // ROUNDS_PER_BATCH, (r % ROUNDS_PER_BATCH) * ROUND_TILES

        def tiles_in_span(r):
            return slice((r % SPAN_ROUNDS) * ROUND_TILES, (r % SPAN_ROUNDS + 1) * ROUND_TILES)

        x_spans = []

        def load_x(span, pieces, table_slots=(), more_pieces=()):
            b, first = batch_and_first_slot(span * SPAN_ROUNDS)
            x_sb = x_pool.tile([P, SPAN_TILES, HIDDEN], BF16, name="x_sb")
            x_spans.append(x_sb)
            t = 0
            for tiles in pieces:
                nc.sync.dma_start(
                    out=x_sb[:, t : t + tiles, :], in_=x_view[b, :, first + t : first + t + tiles, :]
                )
                t += tiles
            for slots in table_slots:
                load_tables(slots)
            for tiles in more_pieces:
                nc.sync.dma_start(
                    out=x_sb[:, t : t + tiles, :], in_=x_view[b, :, first + t : first + t + tiles, :]
                )
                t += tiles

        def store(tile, view, r, cols):
            b, first = batch_and_first_slot(r)
            nc.sync.dma_start(out=view[b, :, first : first + ROUND_TILES, :], in_=tile[:, :, cols])

        w_plane = const.tile([P, OUT_COLS], U8, align_bytes=64)
        nc.vector.memset(w_plane[:].bitcast(I32), 0)
        ident = const.tile([P, P], F32)
        make_identity(nc, ident[:])

        load_x(0, (BANK_TILES,) * (SPAN_TILES // BANK_TILES))
        w_words = const.tile([P, 2 * OUT_COLS], U8, align_bytes=64)
        nc.sync.dma_start(out=w_words[:].bitcast(I32), in_=w_qkv_words[0].bitcast(I32))
        for quadrant in range(4):
            nc.sync.dma_start(
                out=w_plane[32 * quadrant : 32 * quadrant + 4, :].bitcast(I32),
                in_=w_qkv_scales[0, 4 * quadrant : 4 * quadrant + 4, :].bitcast(I32),
            )

        cos_sb = const.tile([P, SLOTS, LANES], BF16)
        sin_sb = const.tile([P, SLOTS, LANES], BF16)

        def load_tables(slots):
            nc.sync.dma_start(out=sin_sb[:, slots, :], in_=sin_view[:, slots, :])
            nc.sync.dma_start(out=cos_sb[:, slots, :], in_=cos_view[:, slots, :])

        load_tables(slice(0, ROUND_TILES))
        load_x(1, (BANK_TILES, BANK_TILES), (slice(ROUND_TILES, SLOTS),), (ROUND_TILES,))
        for span in range(2, SPANS):
            load_x(span, (SPAN_TILES,))

        def build_tables():
            for slots in (slice(0, ROUND_TILES), slice(ROUND_TILES, SLOTS)):
                even_lanes = sin_sb[:, slots, :].rearrange("p t (i two) -> p t i two", two=2)[:, :, :, 0]
                nc.gpsimd.tensor_scalar(
                    out=even_lanes, in0=even_lanes, scalar1=-1.0, scalar2=0.0, op0=MULT, op1=ADD
                )

        grouped_tiles = {}
        code_tiles = {}
        acc_tiles = {}

        def transpose_and_regroup(r):
            x_words = x_spans[r // SPAN_ROUNDS][:, tiles_in_span(r), :].bitcast(F32)
            grouped = work.tile([P, ROUND_TILES, P, 4], BF16, name="grouped", align_bytes=64)
            grouped_words = (
                grouped[:]
                .rearrange("p a r j -> p a (r j)")
                .bitcast(F32)
                .rearrange("p a (r u) -> p a r u", u=2)
            )
            for bank in range(ROUND_BANKS):
                xt = xt_pool.tile([P, BANK_TILES, 2, P], F32, name="xt")
                for a in range(BANK_TILES):
                    for u in range(2):
                        nc.tensor.transpose(
                            xt[:, a, u, :],
                            x_words[:, bank * BANK_TILES + a, u : HIDDEN // 2 : 2],
                            ident[:],
                        )
                nc.scalar.copy(
                    out=grouped_words[:, bank * BANK_TILES : (bank + 1) * BANK_TILES, :, :],
                    in_=xt[:].rearrange("p a u r -> p a r u"),
                )
            grouped_tiles[r] = grouped

        def quantise(r):
            codes = work.tile([P, ROUND_TILES * P], U32, name="codes", align_bytes=64)
            x_plane = work.tile([P, ROUND_TILES * P], U8, name="x_plane", align_bytes=64)
            grouped = grouped_tiles.pop(r)
            nc.vector.quantize_mx(
                out=codes[:].bitcast(FP8X4),
                scales=x_plane[:],
                in_=grouped[:].rearrange("p a r j -> p (a r j)"),
            )
            code_tiles[r] = (codes, x_plane)

        def multiply(r):
            codes, x_plane = code_tiles.pop(r)
            banks = []
            for bank in range(ROUND_BANKS):
                acc = acc_pool.tile([P, BANK_TILES, OUT_COLS], F32, name="acc")
                for a in range(BANK_TILES):
                    tokens = slice((bank * BANK_TILES + a) * P, (bank * BANK_TILES + a + 1) * P)
                    nc.tensor.matmul_mx(
                        out=acc[:, a, :],
                        lhsT=codes[:, tokens].bitcast(FP8X4),
                        lhsT_scale=x_plane[:, tokens],
                        rhs=w_words[:].bitcast(FP4X4),
                        rhs_scale=w_plane[:],
                        start=True,
                        stop=True,
                    )
                banks.append(acc)
            acc_tiles[r] = banks

        span_tiles = {}

        def span_tile(name, r):
            key = (name, r // SPAN_ROUNDS)
            if key not in span_tiles:
                span_tiles[key] = out_pool.tile([P, SPAN_TILES, LANES], F32, name=name, bufs=SPANS)
            return span_tiles[key]

        def store_span(name, view, r):
            if r % SPAN_ROUNDS == SPAN_ROUNDS - 1:
                b, first = batch_and_first_slot(r - r % SPAN_ROUNDS)
                nc.sync.dma_start(
                    out=view[b, :, first : first + SPAN_TILES, :], in_=span_tiles.pop((name, r // SPAN_ROUNDS))[:]
                )

        def copy_and_store_v(r):
            by_span = r < ROUNDS - LONG_RUN_ROUNDS
            if by_span:
                v_sb = span_tile("v_sb", r)
                first_tile = (r % SPAN_ROUNDS) * ROUND_TILES
            else:
                v_sb = out_pool.tile([P, ROUND_TILES, LANES], F32, name="v_late", bufs=LONG_RUN_ROUNDS)
                first_tile = 0
            for bank, acc in enumerate(acc_tiles[r]):
                t = first_tile + bank * BANK_TILES
                nc.scalar.copy(out=v_sb[:, t : t + BANK_TILES, :], in_=acc[:, :, ROPE_COLS:OUT_COLS])
            if by_span:
                store_span("v_sb", v_view, r)
            else:
                store(v_sb, v_view, r, slice(0, LANES))

        joint_tiles = {}

        def gather_and_store_k(r):
            k_sb = span_tile("k_span", r)
            nc.scalar.copy(out=k_sb[:, tiles_in_span(r), :], in_=joint_tiles.pop(r)[:, :, Q_COLS:ROPE_COLS])
            store_span("k_span", k_view, r)

        product_tiles = {}

        def multiply_by_tables(r):
            first = batch_and_first_slot(r)[1]
            shape = [P, BANK_TILES, ROPE_HEADS, PAIRS, 2]
            from_even = work.tile([P, ROUND_TILES, ROPE_COLS], F32, name="from_even")
            from_odd = work.tile([P, ROUND_TILES, ROPE_COLS], F32, name="from_odd")
            product_tiles[r] = (from_even, from_odd)
            banks = acc_tiles.pop(r)
            for bank, acc in enumerate(banks):
                tiles = slice(bank * BANK_TILES, (bank + 1) * BANK_TILES)
                table_slots = slice(first + bank * BANK_TILES, first + (bank + 1) * BANK_TILES)
                pairs = acc[:, :, 0:ROPE_COLS].rearrange(
                    "p a (h i two) -> p a h i two", h=ROPE_HEADS, two=2
                )
                for operand, table, product in (
                    (pairs, cos_sb, from_even),
                    (pairs[:, :, :, :, ::-1], sin_sb, from_odd),
                ):
                    nc.vector.tensor_tensor(
                        out=product[:, tiles, :].rearrange(
                            "p a (h i two) -> p a h i two", h=ROPE_HEADS, two=2
                        ),
                        in0=operand,
                        in1=table[:, table_slots, :]
                        .rearrange("p a (i two) -> p a i two", two=2)
                        .unsqueeze(2)
                        .broadcast_to(shape),
                        op=MULT,
                    )

        def add_and_store(r, engine, together):
            from_even, from_odd = product_tiles.pop(r)
            if together:
                qk_sb = out_pool.tile([P, ROUND_TILES, ROPE_COLS], F32, name="qk_sb")
                engine.tensor_tensor(out=qk_sb[:], in0=from_even[:], in1=from_odd[:], op=ADD)
                store(qk_sb, q_view, r, slice(0, Q_COLS))
                if r < ROUNDS - LATE_ROUNDS:
                    joint_tiles[r] = qk_sb
                else:
                    store(qk_sb, k_view, r, slice(Q_COLS, ROPE_COLS))
            else:
                for name, view, cols in (
                    ("q_sb", q_view, slice(0, Q_COLS)),
                    ("k_sb", k_view, slice(Q_COLS, ROPE_COLS)),
                ):
                    width = cols.stop - cols.start
                    out_sb = out_pool.tile([P, ROUND_TILES, width], F32, name=name, bufs=LONG_RUN_ROUNDS)
                    engine.tensor_tensor(
                        out=out_sb[:], in0=from_even[:, :, cols], in1=from_odd[:, :, cols], op=ADD
                    )
                    store(out_sb, view, r, slice(0, width))

        ctx.enter_context(tc.manual_schedule())
        for step in range(ROUNDS + 3):
            if 2 <= step <= ROUNDS + 1:
                copy_and_store_v(step - 2)
            if 0 <= step - 5 < ROUNDS - LATE_ROUNDS:
                gather_and_store_k(step - 5)
            if step < ROUNDS:
                transpose_and_regroup(step)
            if step == 3:
                build_tables()
            if step >= 3:
                multiply_by_tables(step - 3)
            if 3 <= step < ROUNDS + 3 - VECTOR_ADDS:
                add_and_store(step - 3, nc.gpsimd, step - 3 < ROUNDS - LONG_RUN_ROUNDS)
            if 1 <= step <= ROUNDS:
                quantise(step - 1)
                multiply(step - 1)
        for r in range(ROUNDS - VECTOR_ADDS, ROUNDS):
            add_and_store(r, nc.vector, False)
